import numpy as np
import ml_dtypes


def mxq(x, axis, fmt="e4m3"):
    dtype, down = {"e4m3": (ml_dtypes.float8_e4m3fn, 7), "e5m2": (ml_dtypes.float8_e5m2, 14)}[fmt]
    v = np.moveaxis(np.asarray(x, np.float32).astype(ml_dtypes.bfloat16).astype(np.float64), axis, -1)
    blocks = v.reshape(v.shape[:-1] + (-1, 32))
    amax = np.abs(blocks).max(-1, keepdims=True)
    byte = np.maximum(np.where(amax > 0, np.frexp(amax)[1] - 1 + 127, 0) - down, 1)
    scale = np.exp2(byte - 127.0)
    codes = (blocks / scale).astype(np.float32).astype(dtype).astype(np.float64)
    return np.moveaxis((codes * scale).reshape(v.shape), -1, axis)


WIDE = False


def mx_kscale(k):
    if not WIDE:
        return np.ones(k)
    levels = np.array([10, -10, 5, -5, 0])
    a = np.random.permutation(np.resize(levels, k // 512 * 4)).reshape(k // 512, 4)
    idx = np.arange(k)
    return np.exp2(a[idx // 512, idx % 128 // 32])


BF16 = ml_dtypes.bfloat16


def bf(x):
    return np.asarray(x, np.float32).astype(BF16)


def f64(x):
    return np.asarray(x).astype(np.float64)


B, D, K, STAGES = 512, 16384, 128, 5
EPS = 1e-6


def setup_inputs():
    s = mx_kscale(D)
    p = np.random.standard_normal((K, D))
    p = p / (EPS + np.sqrt((p * p).sum(axis=1, keepdims=True)))
    return {"cls": bf(np.random.standard_normal((B, D)) * 0.5 * s), "proto": bf(p / s)}


def reference(cls, proto):
    x, p = f64(cls), f64(proto)
    dot = mxq(x, 1, "e4m3") @ mxq(p, 1, "e4m3").T
    e = np.exp(dot - dot.max(axis=1, keepdims=True))
    r = e / e.sum(axis=1, keepdims=True)
    m = mxq(r, 0, "e4m3").T @ mxq(x, 0, "e4m3")
    return m / (np.sqrt((m * m).sum(axis=1, keepdims=True)) + EPS)

@@ -1,0 +1,228 @@
+import concourse.mybir as mybir
+from concourse.masks import make_identity
+
+F32 = mybir.dt.float32
+BF16 = mybir.dt.bfloat16
+U32 = mybir.dt.uint32
+U8 = mybir.dt.uint8
+FP8X4 = mybir.dt.float8_e4m3fn_x4
+ACT = mybir.ActivationFunctionType
+ALU = mybir.AluOpType
+AXIS = mybir.AxisListType
+
+P = 128
+PACK = 4
+VECTORS, FEATURES, PROTOS = 512, 16384, 128
+EPS = 1e-6
+FLOPS = 2 * 2 * VECTORS * PROTOS * FEATURES
+
+ROW_GROUPS = VECTORS // P
+CHUNK = 1024
+N_CHUNKS = FEATURES // CHUNK
+K_PASS = P * PACK
+CHUNK_PASSES = CHUNK // K_PASS
+CHUNK_WORDS = CHUNK // 2
+UNIT = 512
+N_UNITS = FEATURES // UNIT
+CHUNK_UNITS = CHUNK // UNIT
+
+CLS_BUFS = 10
+PROTO_BUFS = 4
+SCALAR_UNIT_STRIDE = 6
+STORE = 2 * UNIT
+
+
+def tile_gmm_pa_k_kernel(tc, cls, proto, out):
+    nc = tc.nc
+    cls_rows = cls.rearrange("(p j) d -> p j d", j=ROW_GROUPS)
+
+    with tc.manual_schedule(), tc.tile_pool(name="keep", bufs=1) as keep, tc.tile_pool(
+        name="stream", bufs=2
+    ) as stream, tc.psum_pool(name="dots", bufs=1) as dots, tc.psum_pool(
+        name="banks", bufs=4
+    ) as banks:
+        ident = keep.tile([P, P], F32)
+        make_identity(nc, ident[:])
+        one = keep.tile([P, 1], F32)
+        nc.vector.memset(one[:], 1.0)
+        warm = keep.tile([P, 1], F32)
+        nc.scalar.activation(out=warm[:], in_=one[:], func=ACT.Exp)
+
+        cls_codes = keep.tile([P, FEATURES], U32, align_bytes=64)
+        cls_scales = keep.tile([P, FEATURES], U8, align_bytes=64)
+        dot = []
+        for j in range(ROW_GROUPS):
+            dot_j = dots.tile([P, PROTOS], F32, name="dot%d" % j)
+            dot.append(dot_j)
+
+        cls_chunks = []
+        proto_chunks = []
+        for c in range(N_CHUNKS):
+            cols = slice(c * CHUNK, (c + 1) * CHUNK)
+            proto_chunk = stream.tile([P, CHUNK], BF16, bufs=PROTO_BUFS)
+            nc.sync.dma_start(out=proto_chunk[:], in_=proto[:, cols])
+            proto_chunks.append(proto_chunk)
+            cls_chunk = stream.tile([P, ROW_GROUPS, CHUNK], BF16, bufs=CLS_BUFS)
+            nc.sync.dma_start(out=cls_chunk[:], in_=cls_rows[:, :, cols])
+            cls_chunks.append(cls_chunk)
+
+        def transpose_rows(words, grouped_words):
+            bank = banks.tile([P, CHUNK_WORDS // P, P], F32, tag="bank")
+            for w in range(CHUNK_WORDS // P):
+                nc.tensor.transpose(bank[:, w, :], words[:, w * P : (w + 1) * P], ident[:])
+            nc.scalar.copy(
+                out=grouped_words.rearrange("q (g r u) -> q g r u", g=CHUNK_PASSES, u=2),
+                in_=bank[:].rearrange("q (g u) r -> q g r u", u=2),
+            )
+
+        grouped_cls = {}
+        grouped_proto = {}
+
+        def transpose_chunk(c):
+            by_feature = stream.tile([P, ROW_GROUPS * CHUNK], BF16, align_bytes=64)
+            proto_by_feature = stream.tile([P, CHUNK], BF16, align_bytes=64)
+            transpose_rows(proto_chunks[c][:].bitcast(F32), proto_by_feature[:].bitcast(F32))
+            for j in range(ROW_GROUPS):
+                transpose_rows(
+                    cls_chunks[c][:, j, :].bitcast(F32),
+                    by_feature[:, j * CHUNK : (j + 1) * CHUNK].bitcast(F32),
+                )
+            grouped_cls[c] = by_feature
+            grouped_proto[c] = proto_by_feature
+
+        def add_chunk_to_dot(c):
+            codes = stream.tile([P, ROW_GROUPS * CHUNK_PASSES * P], U32, align_bytes=64)
+            scales = stream.tile([P, ROW_GROUPS * CHUNK_PASSES * P], U8, align_bytes=64)
+            proto_codes = stream.tile([P, CHUNK_PASSES * P], U32, align_bytes=64)
+            proto_scales = stream.tile([P, CHUNK_PASSES * P], U8, align_bytes=64)
+            nc.vector.quantize_mx(
+                out=proto_codes[:].bitcast(FP8X4), scales=proto_scales[:], in_=grouped_proto[c][:]
+            )
+            nc.vector.quantize_mx(
+                out=codes[:].bitcast(FP8X4), scales=scales[:], in_=grouped_cls[c][:]
+            )
+            for j in range(ROW_GROUPS):
+                for g in range(CHUNK_PASSES):
+                    rows = slice((j * CHUNK_PASSES + g) * P, (j * CHUNK_PASSES + g + 1) * P)
+                    protos = slice(g * P, (g + 1) * P)
+                    nc.tensor.matmul_mx(
+                        out=dot[j][:],
+                        lhsT=codes[:, rows].bitcast(FP8X4),
+                        lhsT_scale=scales[:, rows],
+                        rhs=proto_codes[:, protos].bitcast(FP8X4),
+                        rhs_scale=proto_scales[:, protos],
+                        start=(c == 0 and g == 0),
+                        stop=(c == N_CHUNKS - 1 and g == CHUNK_PASSES - 1),
+                    )
+
+        grouped_units = {}
+
+        def regroup_unit(i):
+            first = (i % CHUNK_UNITS) * UNIT
+            rows = cls_chunks[i // CHUNK_UNITS][:, :, first : first + UNIT]
+            by_vector = stream.tile([P, UNIT, PACK], BF16, tag="staging", bufs=4, align_bytes=64)
+            on_scalar = i % SCALAR_UNIT_STRIDE == SCALAR_UNIT_STRIDE - 1
+            copy = nc.scalar.copy if on_scalar else nc.vector.tensor_copy
+            copy(
+                out=by_vector[:].rearrange("p (c i) j -> p c j i", i=4),
+                in_=rows.rearrange("p j (c i) -> p c j i", i=4),
+            )
+            grouped_units[i] = by_vector
+
+        def quantise_unit(i):
+            cols = slice(i * UNIT, (i + 1) * UNIT)
+            nc.vector.quantize_mx(
+                out=cls_codes[:, cols].bitcast(FP8X4),
+                scales=cls_scales[:, cols],
+                in_=grouped_units[i][:].rearrange("p w j -> p (w j)"),
+            )
+
+        transpose_chunk(0)
+        for c in range(N_CHUNKS):
+            if c + 1 < N_CHUNKS:
+                transpose_chunk(c + 1)
+            regroup_unit(c)
+            add_chunk_to_dot(c)
+            if c > 0:
+                quantise_unit(c - 1)
+
+        top = keep.tile([P, ROW_GROUPS], F32)
+        minus_top = keep.tile([P, ROW_GROUPS], F32)
+        expd = keep.tile([P, ROW_GROUPS, PROTOS], F32)
+        exp_sum = keep.tile([P, ROW_GROUPS], F32)
+        inv_sum = keep.tile([P, ROW_GROUPS], F32)
+        resp = keep.tile([P, PROTOS, PACK], BF16, align_bytes=64)
+        resp_codes = keep.tile([P, PROTOS], U32, align_bytes=64)
+        resp_scales = keep.tile([P, PROTOS], U8, align_bytes=64)
+        for j in range(ROW_GROUPS):
+            nc.vector.tensor_reduce(out=top[:, j : j + 1], in_=dot[j][:], axis=AXIS.X, op=ALU.max)
+        nc.vector.tensor_scalar_mul(minus_top[:], top[:], -1.0)
+        for j in range(ROW_GROUPS):
+            nc.scalar.activation(
+                out=expd[:, j, :],
+                in_=dot[j][:],
+                func=ACT.Exp,
+                bias=minus_top[:, j : j + 1],
+                accum_out=exp_sum[:, j : j + 1],
+            )
+        nc.scalar.activation(out=warm[:], in_=one[:], func=ACT.Sqrt)
+        regroup_unit(N_CHUNKS)
+        quantise_unit(N_CHUNKS - 1)
+        nc.vector.reciprocal(inv_sum[:], exp_sum[:])
+        for j in range(ROW_GROUPS):
+            nc.vector.tensor_scalar_mul(resp[:, :, j], expd[:, j, :], inv_sum[:, j : j + 1])
+        nc.vector.quantize_mx(
+            out=resp_codes[:].bitcast(FP8X4),
+            scales=resp_scales[:],
+            in_=resp[:].rearrange("p k j -> p (k j)"),
+        )
+
+        def second_matmul(i):
+            cols = slice(i * UNIT, (i + 1) * UNIT)
+            bank = banks.tile([P, UNIT], F32, tag="bank")
+            nc.tensor.matmul_mx(
+                out=bank[:],
+                lhsT=resp_codes[:].bitcast(FP8X4),
+                lhsT_scale=resp_scales[:],
+                rhs=cls_codes[:, cols].bitcast(FP8X4),
+                rhs_scale=cls_scales[:, cols],
+                start=True,
+                stop=True,
+            )
+            return bank
+
+        square_sums = keep.tile([P, N_UNITS], F32)
+
+        def sum_squares(i):
+            bank = second_matmul(i)
+            squares = stream.tile([P, UNIT], BF16)
+            nc.scalar.activation(
+                out=squares[:], in_=bank[:], func=ACT.Square, accum_out=square_sums[:, i : i + 1]
+            )
+
+        for i in range(N_CHUNKS + 1, N_UNITS + 1):
+            if i < N_UNITS:
+                regroup_unit(i)
+            quantise_unit(i - 1)
+            done = 2 * (i - N_CHUNKS - 1)
+            sum_squares(done)
+            sum_squares(done + 1)
+
+        total = keep.tile([P, 1], F32)
+        norm = keep.tile([P, 1], F32)
+        norm_eps = keep.tile([P, 1], F32)
+        inv_norm = keep.tile([P, 1], F32)
+        nc.vector.reduce_sum(out=total[:], in_=square_sums[:], axis=AXIS.X)
+        nc.scalar.activation(out=norm[:], in_=total[:], func=ACT.Sqrt)
+        nc.vector.tensor_scalar_add(norm_eps[:], norm[:], EPS)
+        nc.vector.reciprocal(inv_norm[:], norm_eps[:])
+
+        for s in range(FEATURES // STORE):
+            scaled = stream.tile([P, STORE], F32, tag="staging", bufs=4, align_bytes=64)
+            left = second_matmul(2 * s)
+            nc.scalar.activation(
+                out=scaled[:, :UNIT], in_=left[:], func=ACT.Copy, scale=inv_norm[:, 0:1]
+            )
+            right = second_matmul(2 * s + 1)
+            nc.vector.tensor_scalar_mul(scaled[:, UNIT:], right[:], inv_norm[:, 0:1])
+            nc.sync.dma_start(out=out[:, s * STORE : (s + 1) * STORE], in_=scaled[:])

@@ -28,7 +28,8 @@ CHUNK_UNITS = CHUNK // UNIT
 
 CLS_BUFS = 10
 PROTO_BUFS = 4
-SCALAR_UNIT_STRIDE = 6
+STAGING_BUFS = 6
+SCALAR_UNITS = (N_CHUNKS + 2, N_CHUNKS + 3)
 STORE = 2 * UNIT
 
 
@@ -117,12 +118,12 @@ def tile_gmm_pa_k_kernel(tc, cls, proto, out):
 
         grouped_units = {}
 
-        def regroup_unit(i):
+        def regroup_unit(i, copy):
             first = (i % CHUNK_UNITS) * UNIT
             rows = cls_chunks[i // CHUNK_UNITS][:, :, first : first + UNIT]
-            by_vector = stream.tile([P, UNIT, PACK], BF16, tag="staging", bufs=4, align_bytes=64)
-            on_scalar = i % SCALAR_UNIT_STRIDE == SCALAR_UNIT_STRIDE - 1
-            copy = nc.scalar.copy if on_scalar else nc.vector.tensor_copy
+            by_vector = stream.tile(
+                [P, UNIT, PACK], BF16, tag="staging", bufs=STAGING_BUFS, align_bytes=64
+            )
             copy(
                 out=by_vector[:].rearrange("p (c i) j -> p c j i", i=4),
                 in_=rows.rearrange("p j (c i) -> p c j i", i=4),
@@ -138,13 +139,15 @@ def tile_gmm_pa_k_kernel(tc, cls, proto, out):
             )
 
         transpose_chunk(0)
+        regroup_unit(0, nc.vector.tensor_copy)
         for c in range(N_CHUNKS):
             if c + 1 < N_CHUNKS:
                 transpose_chunk(c + 1)
-            regroup_unit(c)
+            regroup_unit(c + 1, nc.vector.tensor_copy)
             add_chunk_to_dot(c)
-            if c > 0:
-                quantise_unit(c - 1)
+            quantise_unit(c)
+        for i in SCALAR_UNITS:
+            regroup_unit(i, nc.scalar.copy)
 
         top = keep.tile([P, ROW_GROUPS], F32)
         minus_top = keep.tile([P, ROW_GROUPS], F32)
@@ -166,8 +169,8 @@ def tile_gmm_pa_k_kernel(tc, cls, proto, out):
                 accum_out=exp_sum[:, j : j + 1],
             )
         nc.scalar.activation(out=warm[:], in_=one[:], func=ACT.Sqrt)
-        regroup_unit(N_CHUNKS)
-        quantise_unit(N_CHUNKS - 1)
+        regroup_unit(N_CHUNKS + 1, nc.vector.tensor_copy)
+        quantise_unit(N_CHUNKS)
         nc.vector.reciprocal(inv_sum[:], exp_sum[:])
         for j in range(ROW_GROUPS):
             nc.vector.tensor_scalar_mul(resp[:, :, j], expd[:, j, :], inv_sum[:, j : j + 1])
@@ -200,13 +203,15 @@ def tile_gmm_pa_k_kernel(tc, cls, proto, out):
                 out=squares[:], in_=bank[:], func=ACT.Square, accum_out=square_sums[:, i : i + 1]
             )
 
-        for i in range(N_CHUNKS + 1, N_UNITS + 1):
-            if i < N_UNITS:
-                regroup_unit(i)
+        sum_squares(0)
+        sum_squares(1)
+        for i in range(N_CHUNKS + 2, N_UNITS + 1):
+            if i < N_UNITS and i not in SCALAR_UNITS:
+                regroup_unit(i, nc.vector.tensor_copy)
             quantise_unit(i - 1)
-            done = 2 * (i - N_CHUNKS - 1)
-            sum_squares(done)
-            sum_squares(done + 1)
+            ready = 2 * (i - N_CHUNKS - 1)
+            sum_squares(ready)
+            sum_squares(ready + 1)
 
         total = keep.tile([P, 1], F32)
         norm = keep.tile([P, 1], F32)
@@ -218,7 +223,7 @@ def tile_gmm_pa_k_kernel(tc, cls, proto, out):
         nc.vector.reciprocal(inv_norm[:], norm_eps[:])
 
         for s in range(FEATURES // STORE):
-            scaled = stream.tile([P, STORE], F32, tag="staging", bufs=4, align_bytes=64)
+            scaled = stream.tile([P, STORE], F32, tag="staging", bufs=STAGING_BUFS, align_bytes=64)
             left = second_matmul(2 * s)
             nc.scalar.activation(
                 out=scaled[:, :UNIT], in_=left[:], func=ACT.Copy, scale=inv_norm[:, 0:1]

@@ -60,12 +60,13 @@ def tile_gmm_pa_k_kernel(tc, cls, proto, out):
         proto_chunks = []
         for c in range(N_CHUNKS):
             cols = slice(c * CHUNK, (c + 1) * CHUNK)
+            cls_chunk = stream.tile([P, ROW_GROUPS, CHUNK], BF16, bufs=CLS_BUFS)
+            for j in range(ROW_GROUPS):
+                nc.sync.dma_start(out=cls_chunk[:, j, :], in_=cls_rows[:, j, cols])
+            cls_chunks.append(cls_chunk)
             proto_chunk = stream.tile([P, CHUNK], BF16, bufs=PROTO_BUFS)
             nc.sync.dma_start(out=proto_chunk[:], in_=proto[:, cols])
             proto_chunks.append(proto_chunk)
-            cls_chunk = stream.tile([P, ROW_GROUPS, CHUNK], BF16, bufs=CLS_BUFS)
-            nc.sync.dma_start(out=cls_chunk[:], in_=cls_rows[:, :, cols])
-            cls_chunks.append(cls_chunk)
 
         def transpose_rows(words, grouped_words):
             bank = banks.tile([P, CHUNK_WORDS // P, P], F32, tag="bank")
@@ -82,12 +83,12 @@ def tile_gmm_pa_k_kernel(tc, cls, proto, out):
         def transpose_chunk(c):
             by_feature = stream.tile([P, ROW_GROUPS * CHUNK], BF16, align_bytes=64)
             proto_by_feature = stream.tile([P, CHUNK], BF16, align_bytes=64)
-            transpose_rows(proto_chunks[c][:].bitcast(F32), proto_by_feature[:].bitcast(F32))
             for j in range(ROW_GROUPS):
                 transpose_rows(
                     cls_chunks[c][:, j, :].bitcast(F32),
                     by_feature[:, j * CHUNK : (j + 1) * CHUNK].bitcast(F32),
                 )
+            transpose_rows(proto_chunks[c][:].bitcast(F32), proto_by_feature[:].bitcast(F32))
             grouped_cls[c] = by_feature
             grouped_proto[c] = proto_by_feature
 
@@ -97,10 +98,10 @@ def tile_gmm_pa_k_kernel(tc, cls, proto, out):
             proto_codes = stream.tile([P, CHUNK_PASSES * P], U32, align_bytes=64)
             proto_scales = stream.tile([P, CHUNK_PASSES * P], U8, align_bytes=64)
             nc.vector.quantize_mx(
-                out=proto_codes[:].bitcast(FP8X4), scales=proto_scales[:], in_=grouped_proto[c][:]
+                out=codes[:].bitcast(FP8X4), scales=scales[:], in_=grouped_cls[c][:]
             )
             nc.vector.quantize_mx(
-                out=codes[:].bitcast(FP8X4), scales=scales[:], in_=grouped_cls[c][:]
+                out=proto_codes[:].bitcast(FP8X4), scales=proto_scales[:], in_=grouped_proto[c][:]
             )
             for j in range(ROW_GROUPS):
                 for g in range(CHUNK_PASSES):
@@ -213,11 +214,14 @@ def tile_gmm_pa_k_kernel(tc, cls, proto, out):
             sum_squares(ready)
             sum_squares(ready + 1)
 
+        sums_copy = keep.tile([P, N_UNITS], F32)
         total = keep.tile([P, 1], F32)
         norm = keep.tile([P, 1], F32)
         norm_eps = keep.tile([P, 1], F32)
         inv_norm = keep.tile([P, 1], F32)
-        nc.vector.reduce_sum(out=total[:], in_=square_sums[:], axis=AXIS.X)
+        nc.scalar.activation(
+            out=sums_copy[:], in_=square_sums[:], func=ACT.Copy, accum_out=total[:]
+        )
         nc.scalar.activation(out=norm[:], in_=total[:], func=ACT.Sqrt)
         nc.vector.tensor_scalar_add(norm_eps[:], norm[:], EPS)
         nc.vector.reciprocal(inv_norm[:], norm_eps[:])

@@ -28,8 +28,9 @@ CHUNK_UNITS = CHUNK // UNIT
 
 CLS_BUFS = 10
 PROTO_BUFS = 4
-STAGING_BUFS = 6
-SCALAR_UNITS = (N_CHUNKS + 2, N_CHUNKS + 3)
+STAGING_BUFS = 3
+REGROUPED_EARLY = N_CHUNKS // 2 + 1
+SCALAR_CHUNK = REGROUPED_EARLY
 STORE = 2 * UNIT
 
 
@@ -60,7 +61,7 @@ def tile_gmm_pa_k_kernel(tc, cls, proto, out):
         proto_chunks = []
         for c in range(N_CHUNKS):
             cols = slice(c * CHUNK, (c + 1) * CHUNK)
-            cls_chunk = stream.tile([P, ROW_GROUPS, CHUNK], BF16, bufs=CLS_BUFS)
+            cls_chunk = stream.tile([P, ROW_GROUPS, CHUNK], BF16, tag="cls", bufs=CLS_BUFS)
             for j in range(ROW_GROUPS):
                 nc.sync.dma_start(out=cls_chunk[:, j, :], in_=cls_rows[:, j, cols])
             cls_chunks.append(cls_chunk)
@@ -117,38 +118,37 @@ def tile_gmm_pa_k_kernel(tc, cls, proto, out):
                         stop=(c == N_CHUNKS - 1 and g == CHUNK_PASSES - 1),
                     )
 
-        grouped_units = {}
+        grouped_chunks = {}
 
-        def regroup_unit(i, copy):
-            first = (i % CHUNK_UNITS) * UNIT
-            rows = cls_chunks[i // CHUNK_UNITS][:, :, first : first + UNIT]
+        def regroup_chunk(k, copy):
             by_vector = stream.tile(
-                [P, UNIT, PACK], BF16, tag="staging", bufs=STAGING_BUFS, align_bytes=64
+                [P, CHUNK, PACK], BF16, tag="staging", bufs=STAGING_BUFS, align_bytes=64
             )
             copy(
                 out=by_vector[:].rearrange("p (c i) j -> p c j i", i=4),
-                in_=rows.rearrange("p j (c i) -> p c j i", i=4),
+                in_=cls_chunks[k][:].rearrange("p j (c i) -> p c j i", i=4),
             )
-            grouped_units[i] = by_vector
+            grouped_chunks[k] = by_vector
 
-        def quantise_unit(i):
-            cols = slice(i * UNIT, (i + 1) * UNIT)
+        def quantise_chunk(k):
+            cols = slice(k * CHUNK, (k + 1) * CHUNK)
             nc.vector.quantize_mx(
                 out=cls_codes[:, cols].bitcast(FP8X4),
                 scales=cls_scales[:, cols],
-                in_=grouped_units[i][:].rearrange("p w j -> p (w j)"),
+                in_=grouped_chunks[k][:].rearrange("p w j -> p (w j)"),
             )
 
         transpose_chunk(0)
-        regroup_unit(0, nc.vector.tensor_copy)
+        regroup_chunk(0, nc.vector.tensor_copy)
         for c in range(N_CHUNKS):
             if c + 1 < N_CHUNKS:
                 transpose_chunk(c + 1)
-            regroup_unit(c + 1, nc.vector.tensor_copy)
             add_chunk_to_dot(c)
-            quantise_unit(c)
-        for i in SCALAR_UNITS:
-            regroup_unit(i, nc.scalar.copy)
+            if c % 2 == 0:
+                regroup_chunk(c // 2 + 1, nc.vector.tensor_copy)
+            else:
+                quantise_chunk(c // 2)
+        regroup_chunk(SCALAR_CHUNK, nc.scalar.copy)
 
         top = keep.tile([P, ROW_GROUPS], F32)
         minus_top = keep.tile([P, ROW_GROUPS], F32)
@@ -170,8 +170,7 @@ def tile_gmm_pa_k_kernel(tc, cls, proto, out):
                 accum_out=exp_sum[:, j : j + 1],
             )
         nc.scalar.activation(out=warm[:], in_=one[:], func=ACT.Sqrt)
-        regroup_unit(N_CHUNKS + 1, nc.vector.tensor_copy)
-        quantise_unit(N_CHUNKS)
+        quantise_chunk(REGROUPED_EARLY - 1)
         nc.vector.reciprocal(inv_sum[:], exp_sum[:])
         for j in range(ROW_GROUPS):
             nc.vector.tensor_scalar_mul(resp[:, :, j], expd[:, j, :], inv_sum[:, j : j + 1])
@@ -204,15 +203,14 @@ def tile_gmm_pa_k_kernel(tc, cls, proto, out):
                 out=squares[:], in_=bank[:], func=ACT.Square, accum_out=square_sums[:, i : i + 1]
             )
 
-        sum_squares(0)
-        sum_squares(1)
-        for i in range(N_CHUNKS + 2, N_UNITS + 1):
-            if i < N_UNITS and i not in SCALAR_UNITS:
-                regroup_unit(i, nc.vector.tensor_copy)
-            quantise_unit(i - 1)
-            ready = 2 * (i - N_CHUNKS - 1)
-            sum_squares(ready)
-            sum_squares(ready + 1)
+        for i in range(REGROUPED_EARLY * CHUNK_UNITS):
+            sum_squares(i)
+        for k in range(SCALAR_CHUNK, N_CHUNKS):
+            if k + 1 < N_CHUNKS:
+                regroup_chunk(k + 1, nc.vector.tensor_copy)
+            quantise_chunk(k)
+            for i in range(k * CHUNK_UNITS, (k + 1) * CHUNK_UNITS):
+                sum_squares(i)
 
         sums_copy = keep.tile([P, N_UNITS], F32)
         total = keep.tile([P, 1], F32)
@@ -227,7 +225,7 @@ def tile_gmm_pa_k_kernel(tc, cls, proto, out):
         nc.vector.reciprocal(inv_norm[:], norm_eps[:])
 
         for s in range(FEATURES // STORE):
-            scaled = stream.tile([P, STORE], F32, tag="staging", bufs=STAGING_BUFS, align_bytes=64)
+            scaled = stream.tile([P, STORE], F32, tag="cls", bufs=CLS_BUFS)
             left = second_matmul(2 * s)
             nc.scalar.activation(
                 out=scaled[:, :UNIT], in_=left[:], func=ACT.Copy, scale=inv_norm[:, 0:1]

@@ -125,8 +125,8 @@ def tile_gmm_pa_k_kernel(tc, cls, proto, out):
                 [P, CHUNK, PACK], BF16, tag="staging", bufs=STAGING_BUFS, align_bytes=64
             )
             copy(
-                out=by_vector[:].rearrange("p (c i) j -> p c j i", i=4),
-                in_=cls_chunks[k][:].rearrange("p j (c i) -> p c j i", i=4),
+                out=by_vector[:].rearrange("p (c i) j -> p c j i", i=8),
+                in_=cls_chunks[k][:].rearrange("p j (c i) -> p c j i", i=8),
             )
             grouped_chunks[k] = by_vector
 

import concourse.mybir as mybir
from concourse.masks import make_identity

F32 = mybir.dt.float32
BF16 = mybir.dt.bfloat16
U32 = mybir.dt.uint32
U8 = mybir.dt.uint8
FP8X4 = mybir.dt.float8_e4m3fn_x4
ACT = mybir.ActivationFunctionType
ALU = mybir.AluOpType
AXIS = mybir.AxisListType

P = 128
PACK = 4
VECTORS, FEATURES, PROTOS = 512, 16384, 128
EPS = 1e-6
FLOPS = 2 * 2 * VECTORS * PROTOS * FEATURES

ROW_GROUPS = VECTORS // P
CHUNK = 1024
N_CHUNKS = FEATURES // CHUNK
K_PASS = P * PACK
CHUNK_PASSES = CHUNK // K_PASS
CHUNK_WORDS = CHUNK // 2
UNIT = 512
N_UNITS = FEATURES // UNIT
CHUNK_UNITS = CHUNK // UNIT

CLS_BUFS = 10
PROTO_BUFS = 4
STAGING_BUFS = 3
REGROUPED_EARLY = N_CHUNKS // 2 + 1
SCALAR_CHUNK = REGROUPED_EARLY
STORE = 2 * UNIT


def tile_gmm_pa_k_kernel(tc, cls, proto, out):
    nc = tc.nc
    cls_rows = cls.rearrange("(p j) d -> p j d", j=ROW_GROUPS)

    with tc.manual_schedule(), tc.tile_pool(name="keep", bufs=1) as keep, tc.tile_pool(
        name="stream", bufs=2
    ) as stream, tc.psum_pool(name="dots", bufs=1) as dots, tc.psum_pool(
        name="banks", bufs=4
    ) as banks:
        ident = keep.tile([P, P], F32)
        make_identity(nc, ident[:])
        one = keep.tile([P, 1], F32)
        nc.vector.memset(one[:], 1.0)
        warm = keep.tile([P, 1], F32)
        nc.scalar.activation(out=warm[:], in_=one[:], func=ACT.Exp)

        cls_codes = keep.tile([P, FEATURES], U32, align_bytes=64)
        cls_scales = keep.tile([P, FEATURES], U8, align_bytes=64)
        dot = []
        for j in range(ROW_GROUPS):
            dot_j = dots.tile([P, PROTOS], F32, name="dot%d" % j)
            dot.append(dot_j)

        cls_chunks = []
        proto_chunks = []
        for c in range(N_CHUNKS):
            cols = slice(c * CHUNK, (c + 1) * CHUNK)
            cls_chunk = stream.tile([P, ROW_GROUPS, CHUNK], BF16, tag="cls", bufs=CLS_BUFS)
            for j in range(ROW_GROUPS):
                nc.sync.dma_start(out=cls_chunk[:, j, :], in_=cls_rows[:, j, cols])
            cls_chunks.append(cls_chunk)
            proto_chunk = stream.tile([P, CHUNK], BF16, bufs=PROTO_BUFS)
            nc.sync.dma_start(out=proto_chunk[:], in_=proto[:, cols])
            proto_chunks.append(proto_chunk)

        def transpose_rows(words, grouped_words):
            bank = banks.tile([P, CHUNK_WORDS // P, P], F32, tag="bank")
            for w in range(CHUNK_WORDS // P):
                nc.tensor.transpose(bank[:, w, :], words[:, w * P : (w + 1) * P], ident[:])
            nc.scalar.copy(
                out=grouped_words.rearrange("q (g r u) -> q g r u", g=CHUNK_PASSES, u=2),
                in_=bank[:].rearrange("q (g u) r -> q g r u", u=2),
            )

        grouped_cls = {}
        grouped_proto = {}

        def transpose_chunk(c):
            by_feature = stream.tile([P, ROW_GROUPS * CHUNK], BF16, align_bytes=64)
            proto_by_feature = stream.tile([P, CHUNK], BF16, align_bytes=64)
            for j in range(ROW_GROUPS):
                transpose_rows(
                    cls_chunks[c][:, j, :].bitcast(F32),
                    by_feature[:, j * CHUNK : (j + 1) * CHUNK].bitcast(F32),
                )
            transpose_rows(proto_chunks[c][:].bitcast(F32), proto_by_feature[:].bitcast(F32))
            grouped_cls[c] = by_feature
            grouped_proto[c] = proto_by_feature

        def add_chunk_to_dot(c):
            codes = stream.tile([P, ROW_GROUPS * CHUNK_PASSES * P], U32, align_bytes=64)
            scales = stream.tile([P, ROW_GROUPS * CHUNK_PASSES * P], U8, align_bytes=64)
            proto_codes = stream.tile([P, CHUNK_PASSES * P], U32, align_bytes=64)
            proto_scales = stream.tile([P, CHUNK_PASSES * P], U8, align_bytes=64)
            nc.vector.quantize_mx(
                out=codes[:].bitcast(FP8X4), scales=scales[:], in_=grouped_cls[c][:]
            )
            nc.vector.quantize_mx(
                out=proto_codes[:].bitcast(FP8X4), scales=proto_scales[:], in_=grouped_proto[c][:]
            )
            for j in range(ROW_GROUPS):
                for g in range(CHUNK_PASSES):
                    rows = slice((j * CHUNK_PASSES + g) * P, (j * CHUNK_PASSES + g + 1) * P)
                    protos = slice(g * P, (g + 1) * P)
                    nc.tensor.matmul_mx(
                        out=dot[j][:],
                        lhsT=codes[:, rows].bitcast(FP8X4),
                        lhsT_scale=scales[:, rows],
                        rhs=proto_codes[:, protos].bitcast(FP8X4),
                        rhs_scale=proto_scales[:, protos],
                        start=(c == 0 and g == 0),
                        stop=(c == N_CHUNKS - 1 and g == CHUNK_PASSES - 1),
                    )

        grouped_chunks = {}

        def regroup_chunk(k, copy):
            by_vector = stream.tile(
                [P, CHUNK, PACK], BF16, tag="staging", bufs=STAGING_BUFS, align_bytes=64
            )
            copy(
                out=by_vector[:].rearrange("p (c i) j -> p c j i", i=8),
                in_=cls_chunks[k][:].rearrange("p j (c i) -> p c j i", i=8),
            )
            grouped_chunks[k] = by_vector

        def quantise_chunk(k):
            cols = slice(k * CHUNK, (k + 1) * CHUNK)
            nc.vector.quantize_mx(
                out=cls_codes[:, cols].bitcast(FP8X4),
                scales=cls_scales[:, cols],
                in_=grouped_chunks[k][:].rearrange("p w j -> p (w j)"),
            )

        transpose_chunk(0)
        regroup_chunk(0, nc.vector.tensor_copy)
        for c in range(N_CHUNKS):
            if c + 1 < N_CHUNKS:
                transpose_chunk(c + 1)
            add_chunk_to_dot(c)
            if c % 2 == 0:
                regroup_chunk(c // 2 + 1, nc.vector.tensor_copy)
            else:
                quantise_chunk(c // 2)
        regroup_chunk(SCALAR_CHUNK, nc.scalar.copy)

        top = keep.tile([P, ROW_GROUPS], F32)
        minus_top = keep.tile([P, ROW_GROUPS], F32)
        expd = keep.tile([P, ROW_GROUPS, PROTOS], F32)
        exp_sum = keep.tile([P, ROW_GROUPS], F32)
        inv_sum = keep.tile([P, ROW_GROUPS], F32)
        resp = keep.tile([P, PROTOS, PACK], BF16, align_bytes=64)
        resp_codes = keep.tile([P, PROTOS], U32, align_bytes=64)
        resp_scales = keep.tile([P, PROTOS], U8, align_bytes=64)
        for j in range(ROW_GROUPS):
            nc.vector.tensor_reduce(out=top[:, j : j + 1], in_=dot[j][:], axis=AXIS.X, op=ALU.max)
        nc.vector.tensor_scalar_mul(minus_top[:], top[:], -1.0)
        for j in range(ROW_GROUPS):
            nc.scalar.activation(
                out=expd[:, j, :],
                in_=dot[j][:],
                func=ACT.Exp,
                bias=minus_top[:, j : j + 1],
                accum_out=exp_sum[:, j : j + 1],
            )
        nc.scalar.activation(out=warm[:], in_=one[:], func=ACT.Sqrt)
        quantise_chunk(REGROUPED_EARLY - 1)
        nc.vector.reciprocal(inv_sum[:], exp_sum[:])
        for j in range(ROW_GROUPS):
            nc.vector.tensor_scalar_mul(resp[:, :, j], expd[:, j, :], inv_sum[:, j : j + 1])
        nc.vector.quantize_mx(
            out=resp_codes[:].bitcast(FP8X4),
            scales=resp_scales[:],
            in_=resp[:].rearrange("p k j -> p (k j)"),
        )

        def second_matmul(i):
            cols = slice(i * UNIT, (i + 1) * UNIT)
            bank = banks.tile([P, UNIT], F32, tag="bank")
            nc.tensor.matmul_mx(
                out=bank[:],
                lhsT=resp_codes[:].bitcast(FP8X4),
                lhsT_scale=resp_scales[:],
                rhs=cls_codes[:, cols].bitcast(FP8X4),
                rhs_scale=cls_scales[:, cols],
                start=True,
                stop=True,
            )
            return bank

        square_sums = keep.tile([P, N_UNITS], F32)

        def sum_squares(i):
            bank = second_matmul(i)
            squares = stream.tile([P, UNIT], BF16)
            nc.scalar.activation(
                out=squares[:], in_=bank[:], func=ACT.Square, accum_out=square_sums[:, i : i + 1]
            )

        for i in range(REGROUPED_EARLY * CHUNK_UNITS):
            sum_squares(i)
        for k in range(SCALAR_CHUNK, N_CHUNKS):
            if k + 1 < N_CHUNKS:
                regroup_chunk(k + 1, nc.vector.tensor_copy)
            quantise_chunk(k)
            for i in range(k * CHUNK_UNITS, (k + 1) * CHUNK_UNITS):
                sum_squares(i)

        sums_copy = keep.tile([P, N_UNITS], F32)
        total = keep.tile([P, 1], F32)
        norm = keep.tile([P, 1], F32)
        norm_eps = keep.tile([P, 1], F32)
        inv_norm = keep.tile([P, 1], F32)
        nc.scalar.activation(
            out=sums_copy[:], in_=square_sums[:], func=ACT.Copy, accum_out=total[:]
        )
        nc.scalar.activation(out=norm[:], in_=total[:], func=ACT.Sqrt)
        nc.vector.tensor_scalar_add(norm_eps[:], norm[:], EPS)
        nc.vector.reciprocal(inv_norm[:], norm_eps[:])

        for s in range(FEATURES // STORE):
            scaled = stream.tile([P, STORE], F32, tag="cls", bufs=CLS_BUFS)
            left = second_matmul(2 * s)
            nc.scalar.activation(
                out=scaled[:, :UNIT], in_=left[:], func=ACT.Copy, scale=inv_norm[:, 0:1]
            )
            right = second_matmul(2 * s + 1)
            nc.vector.tensor_scalar_mul(scaled[:, UNIT:], right[:], inv_norm[:, 0:1])
            nc.sync.dma_start(out=out[:, s * STORE : (s + 1) * STORE], in_=scaled[:])
